import numpy as np
import ml_dtypes


def mxq(x, axis, fmt="e4m3"):
    dtype, down = {"e4m3": (ml_dtypes.float8_e4m3fn, 7), "e5m2": (ml_dtypes.float8_e5m2, 14)}[fmt]
    v = np.moveaxis(np.asarray(x, np.float32).astype(ml_dtypes.bfloat16).astype(np.float64), axis, -1)
    blocks = v.reshape(v.shape[:-1] + (-1, 32))
    amax = np.abs(blocks).max(-1, keepdims=True)
    byte = np.maximum(np.where(amax > 0, np.frexp(amax)[1] - 1 + 127, 0) - down, 1)
    scale = np.exp2(byte - 127.0)
    codes = (blocks / scale).astype(np.float32).astype(dtype).astype(np.float64)
    return np.moveaxis((codes * scale).reshape(v.shape), -1, axis)


WIDE = False


def mx_kscale(k):
    if not WIDE:
        return np.ones(k)
    levels = np.array([10, -10, 5, -5, 0])
    a = np.random.permutation(np.resize(levels, k // 512 * 4)).reshape(k // 512, 4)
    idx = np.arange(k)
    return np.exp2(a[idx // 512, idx % 128 // 32])


BF16 = ml_dtypes.bfloat16


def bf(x):
    return np.asarray(x, np.float32).astype(BF16)


def f64(x):
    return np.asarray(x).astype(np.float64)


B, N, DIM, QK, HID = 2, 512, 1024, 128, 2048
EPS = 1e-5
C_SIM = 6.0


def silu(v):
    return v / (1.0 + np.exp(-v))


def setup_inputs():
    s = mx_kscale(DIM)
    r = 10.0 ** np.random.uniform(-2.5, 0.5, (B, N, 1))
    sq = np.sqrt(C_SIM * np.sqrt(N) / np.sqrt(QK))
    return {"x": bf(np.random.standard_normal((B, N, DIM)) * r),
            "ln_scale": bf((1.0 + 0.1 * np.random.standard_normal(DIM)) * s),
            "ln_bias": bf(0.2 * np.random.standard_normal(DIM) * s),
            "W_hidden": bf(np.random.standard_normal((DIM, 2 * HID)) / np.sqrt(DIM) / s[:, None]),
            "b_hidden": bf(0.3 * np.random.standard_normal(2 * HID)),
            "W_qk": bf(np.random.standard_normal((DIM, QK)) / np.sqrt(DIM) / s[:, None]),
            "b_qk": bf(0.3 * np.random.standard_normal(QK)),
            "os_weight": bf(np.random.standard_normal((2, QK)) * sq / 0.6),
            "os_bias": bf(np.random.standard_normal((2, QK)))}


def reference(x, ln_scale, ln_bias, W_hidden, b_hidden, W_qk, b_qk, os_weight, os_bias):
    x = f64(x)
    mu = x.mean(-1, keepdims=True)
    var = np.square(x - mu).mean(-1, keepdims=True)
    xn = (x - mu) / np.sqrt(var + EPS) * f64(ln_scale) + f64(ln_bias)
    xq = mxq(xn, 2, "e4m3")
    hid = silu((xq @ mxq(f64(W_hidden), 0, "e4m3")) + f64(b_hidden))
    v, gate = hid[..., :HID], hid[..., HID:]
    qk = silu((xq @ mxq(f64(W_qk), 0, "e4m3")) + f64(b_qk))
    qk2 = qk[..., None, :] * f64(os_weight) + f64(os_bias)
    return v, gate, qk2[..., 0, :], qk2[..., 1, :]

@@ -1,0 +1,293 @@
+from contextlib import ExitStack
+
+import concourse.mybir as mybir
+from concourse.masks import make_identity
+
+F32 = mybir.dt.float32
+BF16 = mybir.dt.bfloat16
+U32 = mybir.dt.uint32
+U8 = mybir.dt.uint8
+I32 = mybir.dt.int32
+FP8X4 = mybir.dt.float8_e4m3fn_x4
+ALU = mybir.AluOpType
+ACT = mybir.ActivationFunctionType
+
+P = 128
+PACK = 4
+TOKENS = 1024
+DIM = 1024
+HID = 2048
+QK = 128
+EPS = 1e-5
+PASSES = DIM // (P * PACK)
+K_BLOCKS = DIM // P
+TOKEN_TILES = TOKENS // P
+BANK = 512
+HALF_TILES = BANK // P
+HALVES = TOKEN_TILES // HALF_TILES
+BN_WIDTH = 512
+CHUNK = 1024
+CHUNKS = 2 * HID // CHUNK
+RUN = 4
+SCALAR_COLS = 768
+
+B_HIDDEN_AT = 0
+B_QK_AT = 2 * HID
+OS_WEIGHT_AT = B_QK_AT + QK
+OS_BIAS_AT = OS_WEIGHT_AT + 2 * QK
+VEC_COLS = 5 * 1024
+
+FLOPS = 2 * TOKENS * DIM * (2 * HID + QK)
+
+
+def tile_gau_pa_kernel(
+    tc, x, ln_scale, ln_bias, W_hidden, b_hidden, W_qk, b_qk, os_weight, os_bias, out_0, out_1, out_2, out_3
+):
+    nc = tc.nc
+    with ExitStack() as ctx:
+        keep = ctx.enter_context(tc.tile_pool(name="keep", bufs=1))
+        xhat_pool = ctx.enter_context(tc.tile_pool(name="xhat", bufs=HALF_TILES))
+        raw_pool = ctx.enter_context(tc.tile_pool(name="raw", bufs=6))
+        grouped_pool = ctx.enter_context(tc.tile_pool(name="grouped", bufs=2))
+        stage_pool = ctx.enter_context(tc.tile_pool(name="stage", bufs=4))
+        psum = ctx.enter_context(tc.psum_pool(name="psum", bufs=8))
+
+        x_view = x.flatten_outer_dims().rearrange("(p j) d -> p j d", j=TOKEN_TILES)
+        v_view = out_0.flatten_outer_dims().rearrange("(p j) n -> p j n", j=TOKEN_TILES)
+        gate_view = out_1.flatten_outer_dims().rearrange("(p j) n -> p j n", j=TOKEN_TILES)
+        q_view = out_2.flatten_outer_dims().rearrange("(p j) n -> p j n", j=TOKEN_TILES)
+        k_view = out_3.flatten_outer_dims().rearrange("(p j) n -> p j n", j=TOKEN_TILES)
+        w_view = W_hidden.rearrange("(g t p) n -> p g t n", g=PASSES, t=PACK)
+
+        ident_f32 = keep.tile([P, P], F32)
+        make_identity(nc, ident_f32[:])
+        ident_bf16 = keep.tile([P, P], BF16)
+        make_identity(nc, ident_bf16[:])
+        ones = keep.tile([P, P], BF16)
+        nc.vector.memset(ones[:], 1.0)
+        ln_rows = keep.tile([P, P], BF16)
+        nc.vector.memset(ln_rows[:].bitcast(I32), 0)
+        vec_rows = keep.tile([P, VEC_COLS], BF16)
+        nc.vector.memset(vec_rows[:].bitcast(I32), 0)
+
+        x_sb = keep.tile([P, TOKEN_TILES, DIM], BF16)
+        for j in range(0, TOKEN_TILES, 2):
+            nc.sync.dma_start(out=x_sb[:, j : j + 2, :], in_=x_view[:, j : j + 2, :])
+
+        nc.scalar.dma_start(out=ln_rows[0:K_BLOCKS, :], in_=ln_scale.rearrange("(b p) -> b p", p=P))
+        nc.scalar.dma_start(out=ln_rows[K_BLOCKS : 2 * K_BLOCKS, :], in_=ln_bias.rearrange("(b p) -> b p", p=P))
+        nc.scalar.dma_start(out=vec_rows[0:1, B_HIDDEN_AT : B_HIDDEN_AT + 2 * HID], in_=b_hidden.unsqueeze(0))
+        nc.scalar.dma_start(out=vec_rows[0:1, B_QK_AT : B_QK_AT + QK], in_=b_qk.unsqueeze(0))
+        nc.scalar.dma_start(
+            out=vec_rows[0:1, OS_WEIGHT_AT : OS_WEIGHT_AT + 2 * QK],
+            in_=os_weight.rearrange("a n -> (a n)").unsqueeze(0),
+        )
+        nc.scalar.dma_start(
+            out=vec_rows[0:1, OS_BIAS_AT : OS_BIAS_AT + 2 * QK],
+            in_=os_bias.rearrange("a n -> (a n)").unsqueeze(0),
+        )
+
+        w_raw = {}
+
+        def load_chunk(c):
+            for g in range(PASSES):
+                raw = raw_pool.tile([P, PACK, CHUNK], BF16, name="raw")
+                nc.sync.dma_start(out=raw[:], in_=w_view[:, g, :, c * CHUNK : (c + 1) * CHUNK])
+                w_raw[(c, g)] = raw
+
+        load_chunk(0)
+        wqk_raw = keep.tile([P, PASSES * PACK, QK], BF16)
+        nc.sync.dma_start(out=wqk_raw[:], in_=W_qk.rearrange("(s p) n -> p s n", p=P))
+        load_chunk(1)
+        load_chunk(2)
+
+        ln_bank = psum.tile([P, P], BF16, tag="bank")
+        nc.tensor.transpose(ln_bank[:], ln_rows[:], ident_bf16[:])
+        gain_beta = keep.tile([P, 2 * K_BLOCKS], F32)
+        nc.vector.tensor_copy(out=gain_beta[:], in_=ln_bank[:, 0 : 2 * K_BLOCKS])
+
+        vec_all = keep.tile([P, VEC_COLS], BF16)
+        for i in range(VEC_COLS // (2 * BANK)):
+            vec_bank = psum.tile([P, 2 * BANK], BF16, tag="bank")
+            for h in range(2):
+                at = (2 * i + h) * BANK
+                nc.tensor.matmul(
+                    out=vec_bank[:, h * BANK : (h + 1) * BANK],
+                    lhsT=ones[:],
+                    rhs=vec_rows[:, at : at + BANK],
+                    start=True,
+                    stop=True,
+                )
+            nc.scalar.copy(out=vec_all[:, 2 * i * BANK : 2 * (i + 1) * BANK], in_=vec_bank[:])
+
+        stats = keep.tile([P, TOKEN_TILES, DIM // BN_WIDTH, 6], F32)
+        mean_var = keep.tile([P, TOKEN_TILES, 2], F32)
+        var_eps = keep.tile([P, TOKEN_TILES], F32)
+        std = keep.tile([P, TOKEN_TILES], F32)
+        rstd = keep.tile([P, TOKEN_TILES], F32)
+        xn_t = keep.tile([P, K_BLOCKS, TOKENS], BF16)
+        x_codes = keep.tile([P, PASSES, TOKENS], U32, align_bytes=64)
+        x_scales = keep.tile([P, PASSES, TOKENS], U8, align_bytes=64)
+
+        for half in range(HALVES):
+            tiles = range(half * HALF_TILES, (half + 1) * HALF_TILES)
+            cols = slice(half * BANK, (half + 1) * BANK)
+            for j in tiles:
+                for s in range(DIM // BN_WIDTH):
+                    nc.vector.bn_stats(out=stats[:, j, s, :], in_=x_sb[:, j, s * BN_WIDTH : (s + 1) * BN_WIDTH])
+                nc.vector.bn_aggr(out=mean_var[:, j, :], in_=stats[:, j, :, :].rearrange("p s c -> p (s c)"))
+            these = slice(half * HALF_TILES, (half + 1) * HALF_TILES)
+            nc.vector.tensor_scalar(
+                out=var_eps[:, these], in0=mean_var[:, these, 1], scalar1=EPS, scalar2=None, op0=ALU.add
+            )
+            nc.scalar.activation(out=std[:, these], in_=var_eps[:, these], func=ACT.Sqrt)
+            nc.vector.reciprocal(out=rstd[:, these], in_=std[:, these])
+            xhat = []
+            for j in tiles:
+                xh = xhat_pool.tile([P, DIM], F32, name="xh")
+                nc.vector.tensor_scalar(
+                    out=xh[:],
+                    in0=x_sb[:, j, :],
+                    scalar1=mean_var[:, j, 0:1],
+                    scalar2=rstd[:, j : j + 1],
+                    op0=ALU.subtract,
+                    op1=ALU.mult,
+                )
+                xhat.append(xh)
+            for b in range(K_BLOCKS):
+                t_bank = psum.tile([P, HALF_TILES, P], F32, tag="bank")
+                for i in range(HALF_TILES):
+                    nc.tensor.transpose(t_bank[:, i, :], xhat[i][:, b * P : (b + 1) * P], ident_f32[:])
+                nc.scalar.activation(
+                    out=xn_t[:, b, cols],
+                    in_=t_bank[:].rearrange("p i r -> p (i r)"),
+                    func=ACT.Identity,
+                    scale=gain_beta[:, b : b + 1],
+                    bias=gain_beta[:, K_BLOCKS + b : K_BLOCKS + b + 1],
+                )
+            for g in range(PASSES):
+                x_grouped = grouped_pool.tile([P, BANK, PACK], BF16, align_bytes=64)
+                nc.vector.tensor_copy(
+                    out=x_grouped[:].rearrange("p (c i) t -> p c t i", i=RUN),
+                    in_=xn_t[:, g * PACK : (g + 1) * PACK, cols].rearrange("p t (c i) -> p c t i", i=RUN),
+                )
+                nc.vector.quantize_mx(
+                    out=x_codes[:, g, cols].bitcast(FP8X4),
+                    scales=x_scales[:, g, cols],
+                    in_=x_grouped[:].rearrange("p c t -> p (c t)"),
+                )
+
+        w_codes = keep.tile([P, PASSES, 2 * HID], U32, align_bytes=64)
+        w_scales = keep.tile([P, PASSES, 2 * HID], U8, align_bytes=64)
+
+        def prepare(c, g):
+            raw = w_raw[(c, g)]
+            w_grouped = grouped_pool.tile([P, CHUNK, PACK], BF16, align_bytes=64)
+            nc.scalar.copy(
+                out=w_grouped[:, 0:SCALAR_COLS, :].rearrange("p (c i) t -> p c t i", i=RUN),
+                in_=raw[:, :, 0:SCALAR_COLS].rearrange("p t (c i) -> p c t i", i=RUN),
+            )
+            nc.vector.tensor_copy(
+                out=w_grouped[:, SCALAR_COLS:CHUNK, :].rearrange("p (c i) t -> p c t i", i=RUN),
+                in_=raw[:, :, SCALAR_COLS:CHUNK].rearrange("p t (c i) -> p c t i", i=RUN),
+            )
+            nc.vector.quantize_mx(
+                out=w_codes[:, g, c * CHUNK : (c + 1) * CHUNK].bitcast(FP8X4),
+                scales=w_scales[:, g, c * CHUNK : (c + 1) * CHUNK],
+                in_=w_grouped[:].rearrange("p c t -> p (c t)"),
+            )
+
+        wqk_grouped = keep.tile([P, PASSES, QK, PACK], BF16, align_bytes=64)
+        wqk_codes = keep.tile([P, PASSES, QK], U32, align_bytes=64)
+        wqk_scales = keep.tile([P, PASSES, QK], U8, align_bytes=64)
+
+        def prepare_qk():
+            nc.vector.tensor_copy(
+                out=wqk_grouped[:], in_=wqk_raw[:].rearrange("p (g t) n -> p g n t", t=PACK)
+            )
+            nc.vector.quantize_mx(
+                out=wqk_codes[:].rearrange("p g n -> p (g n)").bitcast(FP8X4),
+                scales=wqk_scales[:].rearrange("p g n -> p (g n)"),
+                in_=wqk_grouped[:].rearrange("p g n t -> p (g n t)"),
+            )
+
+        def project(c, j):
+            banks = []
+            for h in range(CHUNK // BANK):
+                acc = psum.tile([P, BANK], F32, tag="bank")
+                banks.append(acc)
+            for g in range(PASSES):
+                for h in range(CHUNK // BANK):
+                    at = c * CHUNK + h * BANK
+                    nc.tensor.matmul_mx(
+                        out=banks[h][:],
+                        lhsT=x_codes[:, g, j * P : (j + 1) * P].bitcast(FP8X4),
+                        lhsT_scale=x_scales[:, g, j * P : (j + 1) * P],
+                        rhs=w_codes[:, g, at : at + BANK].bitcast(FP8X4),
+                        rhs_scale=w_scales[:, g, at : at + BANK],
+                        start=(g == 0),
+                        stop=(g == PASSES - 1),
+                    )
+            stage = stage_pool.tile([P, CHUNK], F32)
+            for h in range(CHUNK // BANK):
+                at = c * CHUNK + h * BANK
+                nc.vector.tensor_tensor(
+                    out=stage[:, h * BANK : (h + 1) * BANK],
+                    in0=banks[h][:],
+                    in1=vec_all[:, B_HIDDEN_AT + at : B_HIDDEN_AT + at + BANK],
+                    op=ALU.add,
+                )
+            nc.scalar.activation(out=stage[:], in_=stage[:], func=ACT.Silu)
+            dest = v_view if c < CHUNKS // 2 else gate_view
+            at = (c % (CHUNKS // 2)) * CHUNK
+            nc.sync.dma_start(out=dest[:, j, at : at + CHUNK], in_=stage[:])
+
+        q_stage = keep.tile([P, TOKEN_TILES, QK], F32)
+        k_stage = keep.tile([P, TOKEN_TILES, QK], F32)
+
+        def along_tiles(at):
+            return vec_all[:, at : at + QK].unsqueeze(1).to_broadcast([P, HALF_TILES, QK])
+
+        def project_qk(half):
+            tiles = slice(half * HALF_TILES, (half + 1) * HALF_TILES)
+            acc = psum.tile([P, HALF_TILES, QK], F32, tag="bank")
+            for i in range(HALF_TILES):
+                j = half * HALF_TILES + i
+                for g in range(PASSES):
+                    nc.tensor.matmul_mx(
+                        out=acc[:, i, :],
+                        lhsT=x_codes[:, g, j * P : (j + 1) * P].bitcast(FP8X4),
+                        lhsT_scale=x_scales[:, g, j * P : (j + 1) * P],
+                        rhs=wqk_codes[:, g, :].bitcast(FP8X4),
+                        rhs_scale=wqk_scales[:, g, :],
+                        start=(g == 0),
+                        stop=(g == PASSES - 1),
+                    )
+            qk = stage_pool.tile([P, HALF_TILES, QK], F32)
+            nc.vector.tensor_tensor(out=qk[:], in0=acc[:], in1=along_tiles(B_QK_AT), op=ALU.add)
+            nc.scalar.activation(out=qk[:], in_=qk[:], func=ACT.Silu)
+            for a, scaled in enumerate((q_stage, k_stage)):
+                nc.gpsimd.tensor_tensor(
+                    out=scaled[:, tiles, :], in0=qk[:], in1=along_tiles(OS_WEIGHT_AT + a * QK), op=ALU.mult
+                )
+                nc.gpsimd.tensor_tensor(
+                    out=scaled[:, tiles, :],
+                    in0=scaled[:, tiles, :],
+                    in1=along_tiles(OS_BIAS_AT + a * QK),
+                    op=ALU.add,
+                )
+
+        for g in range(PASSES):
+            prepare(0, g)
+        prepare_qk()
+        load_chunk(3)
+        for c in range(CHUNKS):
+            for j in range(TOKEN_TILES):
+                if c + 1 < CHUNKS and j % HALF_TILES == 0:
+                    prepare(c + 1, j // HALF_TILES)
+                project(c, j)
+            if c == 0:
+                for half in range(HALVES):
+                    project_qk(half)
+                nc.sync.dma_start(out=q_view, in_=q_stage[:])
+                nc.sync.dma_start(out=k_view, in_=k_stage[:])

@@ -28,8 +28,12 @@ HALVES = TOKEN_TILES // HALF_TILES
 BN_WIDTH = 512
 CHUNK = 1024
 CHUNKS = 2 * HID // CHUNK
+W_TILES = CHUNKS * PASSES
+ROUNDS = CHUNKS * HALVES
+STAGE_BUFS = 7
 RUN = 4
-SCALAR_COLS = 768
+SCALAR_COLS = 512
+GPSIMD_COLS = 128
 
 B_HIDDEN_AT = 0
 B_QK_AT = 2 * HID
@@ -45,11 +49,9 @@ def tile_gau_pa_kernel(
 ):
     nc = tc.nc
     with ExitStack() as ctx:
+        ctx.enter_context(tc.manual_schedule())
         keep = ctx.enter_context(tc.tile_pool(name="keep", bufs=1))
-        xhat_pool = ctx.enter_context(tc.tile_pool(name="xhat", bufs=HALF_TILES))
-        raw_pool = ctx.enter_context(tc.tile_pool(name="raw", bufs=6))
         grouped_pool = ctx.enter_context(tc.tile_pool(name="grouped", bufs=2))
-        stage_pool = ctx.enter_context(tc.tile_pool(name="stage", bufs=4))
         psum = ctx.enter_context(tc.psum_pool(name="psum", bufs=8))
 
         x_view = x.flatten_outer_dims().rearrange("(p j) d -> p j d", j=TOKEN_TILES)
@@ -59,152 +61,74 @@ def tile_gau_pa_kernel(
         k_view = out_3.flatten_outer_dims().rearrange("(p j) n -> p j n", j=TOKEN_TILES)
         w_view = W_hidden.rearrange("(g t p) n -> p g t n", g=PASSES, t=PACK)
 
-        ident_f32 = keep.tile([P, P], F32)
-        make_identity(nc, ident_f32[:])
-        ident_bf16 = keep.tile([P, P], BF16)
-        make_identity(nc, ident_bf16[:])
-        ones = keep.tile([P, P], BF16)
-        nc.vector.memset(ones[:], 1.0)
-        ln_rows = keep.tile([P, P], BF16)
-        nc.vector.memset(ln_rows[:].bitcast(I32), 0)
-        vec_rows = keep.tile([P, VEC_COLS], BF16)
-        nc.vector.memset(vec_rows[:].bitcast(I32), 0)
-
-        x_sb = keep.tile([P, TOKEN_TILES, DIM], BF16)
-        for j in range(0, TOKEN_TILES, 2):
-            nc.sync.dma_start(out=x_sb[:, j : j + 2, :], in_=x_view[:, j : j + 2, :])
-
-        nc.scalar.dma_start(out=ln_rows[0:K_BLOCKS, :], in_=ln_scale.rearrange("(b p) -> b p", p=P))
-        nc.scalar.dma_start(out=ln_rows[K_BLOCKS : 2 * K_BLOCKS, :], in_=ln_bias.rearrange("(b p) -> b p", p=P))
-        nc.scalar.dma_start(out=vec_rows[0:1, B_HIDDEN_AT : B_HIDDEN_AT + 2 * HID], in_=b_hidden.unsqueeze(0))
-        nc.scalar.dma_start(out=vec_rows[0:1, B_QK_AT : B_QK_AT + QK], in_=b_qk.unsqueeze(0))
-        nc.scalar.dma_start(
-            out=vec_rows[0:1, OS_WEIGHT_AT : OS_WEIGHT_AT + 2 * QK],
-            in_=os_weight.rearrange("a n -> (a n)").unsqueeze(0),
-        )
-        nc.scalar.dma_start(
-            out=vec_rows[0:1, OS_BIAS_AT : OS_BIAS_AT + 2 * QK],
-            in_=os_bias.rearrange("a n -> (a n)").unsqueeze(0),
-        )
-
-        w_raw = {}
-
-        def load_chunk(c):
-            for g in range(PASSES):
-                raw = raw_pool.tile([P, PACK, CHUNK], BF16, name="raw")
-                nc.sync.dma_start(out=raw[:], in_=w_view[:, g, :, c * CHUNK : (c + 1) * CHUNK])
-                w_raw[(c, g)] = raw
-
-        load_chunk(0)
-        wqk_raw = keep.tile([P, PASSES * PACK, QK], BF16)
-        nc.sync.dma_start(out=wqk_raw[:], in_=W_qk.rearrange("(s p) n -> p s n", p=P))
-        load_chunk(1)
-        load_chunk(2)
-
-        ln_bank = psum.tile([P, P], BF16, tag="bank")
-        nc.tensor.transpose(ln_bank[:], ln_rows[:], ident_bf16[:])
-        gain_beta = keep.tile([P, 2 * K_BLOCKS], F32)
-        nc.vector.tensor_copy(out=gain_beta[:], in_=ln_bank[:, 0 : 2 * K_BLOCKS])
-
         vec_all = keep.tile([P, VEC_COLS], BF16)
-        for i in range(VEC_COLS // (2 * BANK)):
-            vec_bank = psum.tile([P, 2 * BANK], BF16, tag="bank")
-            for h in range(2):
-                at = (2 * i + h) * BANK
-                nc.tensor.matmul(
-                    out=vec_bank[:, h * BANK : (h + 1) * BANK],
-                    lhsT=ones[:],
-                    rhs=vec_rows[:, at : at + BANK],
-                    start=True,
-                    stop=True,
-                )
-            nc.scalar.copy(out=vec_all[:, 2 * i * BANK : 2 * (i + 1) * BANK], in_=vec_bank[:])
-
-        stats = keep.tile([P, TOKEN_TILES, DIM // BN_WIDTH, 6], F32)
-        mean_var = keep.tile([P, TOKEN_TILES, 2], F32)
-        var_eps = keep.tile([P, TOKEN_TILES], F32)
-        std = keep.tile([P, TOKEN_TILES], F32)
-        rstd = keep.tile([P, TOKEN_TILES], F32)
         xn_t = keep.tile([P, K_BLOCKS, TOKENS], BF16)
         x_codes = keep.tile([P, PASSES, TOKENS], U32, align_bytes=64)
         x_scales = keep.tile([P, PASSES, TOKENS], U8, align_bytes=64)
-
-        for half in range(HALVES):
-            tiles = range(half * HALF_TILES, (half + 1) * HALF_TILES)
-            cols = slice(half * BANK, (half + 1) * BANK)
-            for j in tiles:
-                for s in range(DIM // BN_WIDTH):
-                    nc.vector.bn_stats(out=stats[:, j, s, :], in_=x_sb[:, j, s * BN_WIDTH : (s + 1) * BN_WIDTH])
-                nc.vector.bn_aggr(out=mean_var[:, j, :], in_=stats[:, j, :, :].rearrange("p s c -> p (s c)"))
-            these = slice(half * HALF_TILES, (half + 1) * HALF_TILES)
-            nc.vector.tensor_scalar(
-                out=var_eps[:, these], in0=mean_var[:, these, 1], scalar1=EPS, scalar2=None, op0=ALU.add
-            )
-            nc.scalar.activation(out=std[:, these], in_=var_eps[:, these], func=ACT.Sqrt)
-            nc.vector.reciprocal(out=rstd[:, these], in_=std[:, these])
-            xhat = []
-            for j in tiles:
-                xh = xhat_pool.tile([P, DIM], F32, name="xh")
-                nc.vector.tensor_scalar(
-                    out=xh[:],
-                    in0=x_sb[:, j, :],
-                    scalar1=mean_var[:, j, 0:1],
-                    scalar2=rstd[:, j : j + 1],
-                    op0=ALU.subtract,
-                    op1=ALU.mult,
-                )
-                xhat.append(xh)
-            for b in range(K_BLOCKS):
-                t_bank = psum.tile([P, HALF_TILES, P], F32, tag="bank")
-                for i in range(HALF_TILES):
-                    nc.tensor.transpose(t_bank[:, i, :], xhat[i][:, b * P : (b + 1) * P], ident_f32[:])
-                nc.scalar.activation(
-                    out=xn_t[:, b, cols],
-                    in_=t_bank[:].rearrange("p i r -> p (i r)"),
-                    func=ACT.Identity,
-                    scale=gain_beta[:, b : b + 1],
-                    bias=gain_beta[:, K_BLOCKS + b : K_BLOCKS + b + 1],
-                )
-            for g in range(PASSES):
-                x_grouped = grouped_pool.tile([P, BANK, PACK], BF16, align_bytes=64)
-                nc.vector.tensor_copy(
-                    out=x_grouped[:].rearrange("p (c i) t -> p c t i", i=RUN),
-                    in_=xn_t[:, g * PACK : (g + 1) * PACK, cols].rearrange("p t (c i) -> p c t i", i=RUN),
-                )
-                nc.vector.quantize_mx(
-                    out=x_codes[:, g, cols].bitcast(FP8X4),
-                    scales=x_scales[:, g, cols],
-                    in_=x_grouped[:].rearrange("p c t -> p (c t)"),
-                )
-
         w_codes = keep.tile([P, PASSES, 2 * HID], U32, align_bytes=64)
         w_scales = keep.tile([P, PASSES, 2 * HID], U8, align_bytes=64)
-
-        def prepare(c, g):
-            raw = w_raw[(c, g)]
-            w_grouped = grouped_pool.tile([P, CHUNK, PACK], BF16, align_bytes=64)
-            nc.scalar.copy(
-                out=w_grouped[:, 0:SCALAR_COLS, :].rearrange("p (c i) t -> p c t i", i=RUN),
-                in_=raw[:, :, 0:SCALAR_COLS].rearrange("p t (c i) -> p c t i", i=RUN),
-            )
-            nc.vector.tensor_copy(
-                out=w_grouped[:, SCALAR_COLS:CHUNK, :].rearrange("p (c i) t -> p c t i", i=RUN),
-                in_=raw[:, :, SCALAR_COLS:CHUNK].rearrange("p t (c i) -> p c t i", i=RUN),
-            )
-            nc.vector.quantize_mx(
-                out=w_codes[:, g, c * CHUNK : (c + 1) * CHUNK].bitcast(FP8X4),
-                scales=w_scales[:, g, c * CHUNK : (c + 1) * CHUNK],
-                in_=w_grouped[:].rearrange("p c t -> p (c t)"),
-            )
-
+        wqk_raw = keep.tile([P, PASSES * PACK, QK], BF16)
         wqk_grouped = keep.tile([P, PASSES, QK, PACK], BF16, align_bytes=64)
         wqk_codes = keep.tile([P, PASSES, QK], U32, align_bytes=64)
         wqk_scales = keep.tile([P, PASSES, QK], U8, align_bytes=64)
+        qk = keep.tile([P, TOKEN_TILES, QK], F32)
+        q_stage = keep.tile([P, TOKEN_TILES, QK], F32)
+        k_stage = keep.tile([P, TOKEN_TILES, QK], F32)
+        w_raw = {}
+        w_grouped = {}
+        x_grouped = {}
+
+        def group_x(half, g):
+            grouped = grouped_pool.tile([P, BANK, PACK], BF16, name="x_grouped", align_bytes=64)
+            nc.vector.tensor_copy(
+                out=grouped[:].rearrange("p (c i) t -> p c t i", i=RUN),
+                in_=xn_t[:, g * PACK : (g + 1) * PACK, half * BANK : (half + 1) * BANK].rearrange(
+                    "p t (c i) -> p c t i", i=RUN
+                ),
+            )
+            x_grouped[(half, g)] = grouped
+
+        def quantise_x(half, g):
+            nc.vector.quantize_mx(
+                out=x_codes[:, g, half * BANK : (half + 1) * BANK].bitcast(FP8X4),
+                scales=x_scales[:, g, half * BANK : (half + 1) * BANK],
+                in_=x_grouped[(half, g)][:].rearrange("p c t -> p (c t)"),
+            )
+
+        def load_w(w):
+            c, g = w // PASSES, w % PASSES
+            raw = keep.tile([P, PACK, CHUNK], BF16, name="raw%d" % w)
+            nc.sync.dma_start(out=raw[:], in_=w_view[:, g, :, c * CHUNK : (c + 1) * CHUNK])
+            w_raw[w] = raw
+
+        def regroup_w(w):
+            raw = w_raw[w]
+            grouped = grouped_pool.tile([P, CHUNK, PACK], BF16, name="w_grouped", align_bytes=64)
+            nc.scalar.copy(
+                out=grouped[:, 0:SCALAR_COLS, :].rearrange("p (c i) t -> p c t i", i=RUN),
+                in_=raw[:, :, 0:SCALAR_COLS].rearrange("p t (c i) -> p c t i", i=RUN),
+            )
+            for lo in range(SCALAR_COLS, CHUNK, GPSIMD_COLS):
+                nc.gpsimd.tensor_scalar(
+                    out=grouped[:, lo : lo + GPSIMD_COLS, :],
+                    in0=raw[:, :, lo : lo + GPSIMD_COLS].rearrange("p t c -> p c t"),
+                    scalar1=1.0,
+                    scalar2=0.0,
+                    op0=ALU.mult,
+                    op1=ALU.add,
+                )
+            w_grouped[w] = grouped
+
+        def quantise_w(w):
+            c, g = w // PASSES, w % PASSES
+            nc.vector.quantize_mx(
+                out=w_codes[:, g, c * CHUNK : (c + 1) * CHUNK].bitcast(FP8X4),
+                scales=w_scales[:, g, c * CHUNK : (c + 1) * CHUNK],
+                in_=w_grouped[w][:].rearrange("p c t -> p (c t)"),
+            )
 
         def prepare_qk():
-            nc.vector.tensor_copy(
-                out=wqk_grouped[:], in_=wqk_raw[:].rearrange("p (g t) n -> p g n t", t=PACK)
-            )
+            nc.vector.tensor_copy(out=wqk_grouped[:], in_=wqk_raw[:].rearrange("p (g t) n -> p g n t", t=PACK))
             nc.vector.quantize_mx(
                 out=wqk_codes[:].rearrange("p g n -> p (g n)").bitcast(FP8X4),
                 scales=wqk_scales[:].rearrange("p g n -> p (g n)"),
@@ -242,14 +166,11 @@ def tile_gau_pa_kernel(
             at = (c % (CHUNKS // 2)) * CHUNK
             nc.sync.dma_start(out=dest[:, j, at : at + CHUNK], in_=stage[:])
 
-        q_stage = keep.tile([P, TOKEN_TILES, QK], F32)
-        k_stage = keep.tile([P, TOKEN_TILES, QK], F32)
-
         def along_tiles(at):
             return vec_all[:, at : at + QK].unsqueeze(1).to_broadcast([P, HALF_TILES, QK])
 
         def project_qk(half):
-            tiles = slice(half * HALF_TILES, (half + 1) * HALF_TILES)
+            these = slice(half * HALF_TILES, (half + 1) * HALF_TILES)
             acc = psum.tile([P, HALF_TILES, QK], F32, tag="bank")
             for i in range(HALF_TILES):
                 j = half * HALF_TILES + i
@@ -263,31 +184,168 @@ def tile_gau_pa_kernel(
                         start=(g == 0),
                         stop=(g == PASSES - 1),
                     )
-            qk = stage_pool.tile([P, HALF_TILES, QK], F32)
-            nc.vector.tensor_tensor(out=qk[:], in0=acc[:], in1=along_tiles(B_QK_AT), op=ALU.add)
-            nc.scalar.activation(out=qk[:], in_=qk[:], func=ACT.Silu)
+            nc.vector.tensor_tensor(out=qk[:, these, :], in0=acc[:], in1=along_tiles(B_QK_AT), op=ALU.add)
+            nc.scalar.activation(out=qk[:, these, :], in_=qk[:, these, :], func=ACT.Silu)
+
+        def offset_scale(half):
+            these = slice(half * HALF_TILES, (half + 1) * HALF_TILES)
             for a, scaled in enumerate((q_stage, k_stage)):
                 nc.gpsimd.tensor_tensor(
-                    out=scaled[:, tiles, :], in0=qk[:], in1=along_tiles(OS_WEIGHT_AT + a * QK), op=ALU.mult
+                    out=scaled[:, these, :], in0=qk[:, these, :], in1=along_tiles(OS_WEIGHT_AT + a * QK), op=ALU.mult
                 )
                 nc.gpsimd.tensor_tensor(
-                    out=scaled[:, tiles, :],
-                    in0=scaled[:, tiles, :],
+                    out=scaled[:, these, :],
+                    in0=scaled[:, these, :],
                     in1=along_tiles(OS_BIAS_AT + a * QK),
                     op=ALU.add,
                 )
 
-        for g in range(PASSES):
-            prepare(0, g)
-        prepare_qk()
-        load_chunk(3)
-        for c in range(CHUNKS):
-            for j in range(TOKEN_TILES):
-                if c + 1 < CHUNKS and j % HALF_TILES == 0:
-                    prepare(c + 1, j // HALF_TILES)
-                project(c, j)
-            if c == 0:
-                for half in range(HALVES):
-                    project_qk(half)
-                nc.sync.dma_start(out=q_view, in_=q_stage[:])
-                nc.sync.dma_start(out=k_view, in_=k_stage[:])
+        with tc.tile_pool(name="norm", bufs=1) as norm_pool:
+            ident_bf16 = norm_pool.tile([P, P], BF16)
+            make_identity(nc, ident_bf16[:])
+            ident_f32 = norm_pool.tile([P, P], F32)
+            make_identity(nc, ident_f32[:])
+            ln_rows = norm_pool.tile([P, P], BF16)
+            nc.vector.memset(ln_rows[:].bitcast(I32), 0)
+            vec_rows = norm_pool.tile([P, VEC_COLS], BF16)
+            nc.vector.memset(vec_rows[:].bitcast(I32), 0)
+            ones = norm_pool.tile([P, P], BF16)
+            nc.vector.memset(ones[:], 1.0)
+
+            x_sb = norm_pool.tile([P, TOKEN_TILES, DIM], BF16)
+
+            def load_x(j):
+                nc.sync.dma_start(out=x_sb[:, j : j + 2, :], in_=x_view[:, j : j + 2, :])
+
+            nc.sync.dma_start(out=ln_rows[0:K_BLOCKS, :], in_=ln_scale.rearrange("(b p) -> b p", p=P))
+            nc.sync.dma_start(out=ln_rows[K_BLOCKS : 2 * K_BLOCKS, :], in_=ln_bias.rearrange("(b p) -> b p", p=P))
+            load_x(0)
+            load_x(2)
+            nc.sync.dma_start(out=vec_rows[0:1, B_HIDDEN_AT : B_HIDDEN_AT + 2 * HID], in_=b_hidden.unsqueeze(0))
+            nc.sync.dma_start(out=vec_rows[0:1, B_QK_AT : B_QK_AT + QK], in_=b_qk.unsqueeze(0))
+            nc.sync.dma_start(
+                out=vec_rows[0:1, OS_WEIGHT_AT : OS_WEIGHT_AT + 2 * QK],
+                in_=os_weight.rearrange("a n -> (a n)").unsqueeze(0),
+            )
+            nc.sync.dma_start(
+                out=vec_rows[0:1, OS_BIAS_AT : OS_BIAS_AT + 2 * QK],
+                in_=os_bias.rearrange("a n -> (a n)").unsqueeze(0),
+            )
+            load_x(4)
+            load_x(6)
+            load_w(0)
+            load_w(1)
+            nc.sync.dma_start(out=wqk_raw[:], in_=W_qk.rearrange("(s p) n -> p s n", p=P))
+            for w in range(2, W_TILES):
+                load_w(w)
+
+            ln_bank = psum.tile([P, P], BF16, tag="bank")
+            nc.tensor.transpose(ln_bank[:], ln_rows[:], ident_bf16[:])
+            gain_beta = norm_pool.tile([P, 2 * K_BLOCKS], F32)
+            nc.scalar.copy(out=gain_beta[:], in_=ln_bank[:, 0 : 2 * K_BLOCKS])
+
+            def spread_vectors():
+                for i in range(VEC_COLS // (2 * BANK)):
+                    vec_bank = psum.tile([P, 2 * BANK], BF16, tag="bank")
+                    for h in range(2):
+                        at = (2 * i + h) * BANK
+                        nc.tensor.matmul(
+                            out=vec_bank[:, h * BANK : (h + 1) * BANK],
+                            lhsT=ones[:],
+                            rhs=vec_rows[:, at : at + BANK],
+                            start=True,
+                            stop=True,
+                        )
+                    nc.scalar.copy(out=vec_all[:, 2 * i * BANK : 2 * (i + 1) * BANK], in_=vec_bank[:])
+
+            stats = norm_pool.tile([P, TOKEN_TILES, DIM // BN_WIDTH, 6], F32)
+            mean_var = norm_pool.tile([P, TOKEN_TILES, 2], F32)
+            var_eps = norm_pool.tile([P, TOKEN_TILES], F32)
+            std = norm_pool.tile([P, TOKEN_TILES], F32)
+            rstd = norm_pool.tile([P, TOKEN_TILES], F32)
+
+            def tile_stats(j):
+                for s in range(DIM // BN_WIDTH):
+                    nc.vector.bn_stats(out=stats[:, j, s, :], in_=x_sb[:, j, s * BN_WIDTH : (s + 1) * BN_WIDTH])
+                nc.vector.bn_aggr(out=mean_var[:, j, :], in_=stats[:, j, :, :].rearrange("p s c -> p (s c)"))
+
+            def start_rstd(half):
+                these = slice(half * HALF_TILES, (half + 1) * HALF_TILES)
+                nc.vector.tensor_scalar(
+                    out=var_eps[:, these], in0=mean_var[:, these, 1], scalar1=EPS, scalar2=None, op0=ALU.add
+                )
+                nc.scalar.activation(out=std[:, these], in_=var_eps[:, these], func=ACT.Sqrt)
+
+            def normalise(half):
+                these = slice(half * HALF_TILES, (half + 1) * HALF_TILES)
+                nc.vector.reciprocal(out=rstd[:, these], in_=std[:, these])
+                xhat = []
+                for j in range(half * HALF_TILES, (half + 1) * HALF_TILES):
+                    xh = norm_pool.tile([P, DIM], F32, name="xh", bufs=HALF_TILES)
+                    nc.vector.tensor_scalar(
+                        out=xh[:],
+                        in0=x_sb[:, j, :],
+                        scalar1=mean_var[:, j, 0:1],
+                        scalar2=rstd[:, j : j + 1],
+                        op0=ALU.subtract,
+                        op1=ALU.mult,
+                    )
+                    xhat.append(xh)
+                for b in range(K_BLOCKS):
+                    t_bank = psum.tile([P, HALF_TILES, P], F32, tag="bank")
+                    for i in range(HALF_TILES):
+                        nc.tensor.transpose(t_bank[:, i, :], xhat[i][:, b * P : (b + 1) * P], ident_f32[:])
+                    nc.scalar.activation(
+                        out=xn_t[:, b, half * BANK : (half + 1) * BANK],
+                        in_=t_bank[:].rearrange("p i r -> p (i r)"),
+                        func=ACT.Identity,
+                        scale=gain_beta[:, b : b + 1],
+                        bias=gain_beta[:, K_BLOCKS + b : K_BLOCKS + b + 1],
+                    )
+
+            for j in range(HALF_TILES):
+                tile_stats(j)
+            start_rstd(0)
+            spread_vectors()
+            tile_stats(HALF_TILES)
+            regroup_w(0)
+            normalise(0)
+            for j in range(HALF_TILES + 1, TOKEN_TILES):
+                tile_stats(j)
+            start_rstd(1)
+            regroup_w(1)
+            quantise_w(0)
+            group_x(0, 0)
+            normalise(1)
+            group_x(0, 1)
+            quantise_x(0, 0)
+            quantise_x(0, 1)
+            quantise_w(1)
+            regroup_w(2)
+            prepare_qk()
+
+        stage_pool = ctx.enter_context(tc.tile_pool(name="stage", bufs=STAGE_BUFS))
+
+        for r in range(ROUNDS):
+            c, half = r // HALVES, r % HALVES
+            first = half * HALF_TILES
+            if r + 3 < W_TILES:
+                regroup_w(r + 3)
+            if r % 2 == 1 and r // 2 < HALVES:
+                offset_scale(r // 2)
+            if r == 2 * HALVES - 1:
+                nc.gpsimd.dma_start(out=q_view, in_=q_stage[:])
+                nc.gpsimd.dma_start(out=k_view, in_=k_stage[:])
+            project(c, first)
+            project(c, first + 1)
+            if r == 0:
+                for g in range(PASSES):
+                    group_x(1, g)
+                for g in range(PASSES):
+                    quantise_x(1, g)
+            if r + 2 < W_TILES:
+                quantise_w(r + 2)
+            project(c, first + 2)
+            project(c, first + 3)
+            if r % 2 == 0 and r // 2 < HALVES:
+                project_qk(r // 2)

@@ -62,7 +62,10 @@ def tile_gau_pa_kernel(
         w_view = W_hidden.rearrange("(g t p) n -> p g t n", g=PASSES, t=PACK)
 
         vec_all = keep.tile([P, VEC_COLS], BF16)
-        xn_t = keep.tile([P, K_BLOCKS, TOKENS], BF16)
+        xn_t = []
+        for half in range(HALVES):
+            xn_half = keep.tile([P, K_BLOCKS, BANK], BF16, name="xn_t%d" % half)
+            xn_t.append(xn_half)
         x_codes = keep.tile([P, PASSES, TOKENS], U32, align_bytes=64)
         x_scales = keep.tile([P, PASSES, TOKENS], U8, align_bytes=64)
         w_codes = keep.tile([P, PASSES, 2 * HID], U32, align_bytes=64)
@@ -82,9 +85,7 @@ def tile_gau_pa_kernel(
             grouped = grouped_pool.tile([P, BANK, PACK], BF16, name="x_grouped", align_bytes=64)
             nc.vector.tensor_copy(
                 out=grouped[:].rearrange("p (c i) t -> p c t i", i=RUN),
-                in_=xn_t[:, g * PACK : (g + 1) * PACK, half * BANK : (half + 1) * BANK].rearrange(
-                    "p t (c i) -> p c t i", i=RUN
-                ),
+                in_=xn_t[half][:, g * PACK : (g + 1) * PACK, :].rearrange("p t (c i) -> p c t i", i=RUN),
             )
             x_grouped[(half, g)] = grouped
 
@@ -135,7 +136,7 @@ def tile_gau_pa_kernel(
                 in_=wqk_grouped[:].rearrange("p g n t -> p (g n t)"),
             )
 
-        def project(c, j):
+        def project(c, j, pieces=1):
             banks = []
             for h in range(CHUNK // BANK):
                 acc = psum.tile([P, BANK], F32, tag="bank")
@@ -161,10 +162,12 @@ def tile_gau_pa_kernel(
                     in1=vec_all[:, B_HIDDEN_AT + at : B_HIDDEN_AT + at + BANK],
                     op=ALU.add,
                 )
-            nc.scalar.activation(out=stage[:], in_=stage[:], func=ACT.Silu)
             dest = v_view if c < CHUNKS // 2 else gate_view
             at = (c % (CHUNKS // 2)) * CHUNK
-            nc.sync.dma_start(out=dest[:, j, at : at + CHUNK], in_=stage[:])
+            width = CHUNK // pieces
+            for lo in range(0, CHUNK, width):
+                nc.scalar.activation(out=stage[:, lo : lo + width], in_=stage[:, lo : lo + width], func=ACT.Silu)
+                nc.sync.dma_start(out=dest[:, j, at + lo : at + lo + width], in_=stage[:, lo : lo + width])
 
         def along_tiles(at):
             return vec_all[:, at : at + QK].unsqueeze(1).to_broadcast([P, HALF_TILES, QK])
@@ -201,6 +204,12 @@ def tile_gau_pa_kernel(
                 )
 
         with tc.tile_pool(name="norm", bufs=1) as norm_pool:
+            warm = norm_pool.tile([P, 1], F32)
+            nc.vector.memset(warm[:], 1.0)
+            warm_sqrt = norm_pool.tile([P, 1], F32)
+            nc.scalar.activation(out=warm_sqrt[:], in_=warm[:], func=ACT.Sqrt)
+            warm_silu = norm_pool.tile([P, 1], F32)
+
             ident_bf16 = norm_pool.tile([P, P], BF16)
             make_identity(nc, ident_bf16[:])
             ident_f32 = norm_pool.tile([P, P], F32)
@@ -214,13 +223,14 @@ def tile_gau_pa_kernel(
 
             x_sb = norm_pool.tile([P, TOKEN_TILES, DIM], BF16)
 
-            def load_x(j):
-                nc.sync.dma_start(out=x_sb[:, j : j + 2, :], in_=x_view[:, j : j + 2, :])
+            def load_x(j, tiles):
+                nc.sync.dma_start(out=x_sb[:, j : j + tiles, :], in_=x_view[:, j : j + tiles, :])
 
+            load_x(0, 1)
+            load_x(1, 1)
             nc.sync.dma_start(out=ln_rows[0:K_BLOCKS, :], in_=ln_scale.rearrange("(b p) -> b p", p=P))
             nc.sync.dma_start(out=ln_rows[K_BLOCKS : 2 * K_BLOCKS, :], in_=ln_bias.rearrange("(b p) -> b p", p=P))
-            load_x(0)
-            load_x(2)
+            load_x(2, 2)
             nc.sync.dma_start(out=vec_rows[0:1, B_HIDDEN_AT : B_HIDDEN_AT + 2 * HID], in_=b_hidden.unsqueeze(0))
             nc.sync.dma_start(out=vec_rows[0:1, B_QK_AT : B_QK_AT + QK], in_=b_qk.unsqueeze(0))
             nc.sync.dma_start(
@@ -231,8 +241,8 @@ def tile_gau_pa_kernel(
                 out=vec_rows[0:1, OS_BIAS_AT : OS_BIAS_AT + 2 * QK],
                 in_=os_bias.rearrange("a n -> (a n)").unsqueeze(0),
             )
-            load_x(4)
-            load_x(6)
+            load_x(4, 2)
+            load_x(6, 2)
             load_w(0)
             load_w(1)
             nc.sync.dma_start(out=wqk_raw[:], in_=W_qk.rearrange("(s p) n -> p s n", p=P))
@@ -296,7 +306,7 @@ def tile_gau_pa_kernel(
                     for i in range(HALF_TILES):
                         nc.tensor.transpose(t_bank[:, i, :], xhat[i][:, b * P : (b + 1) * P], ident_f32[:])
                     nc.scalar.activation(
-                        out=xn_t[:, b, half * BANK : (half + 1) * BANK],
+                        out=xn_t[half][:, b, :],
                         in_=t_bank[:].rearrange("p i r -> p (i r)"),
                         func=ACT.Identity,
                         scale=gain_beta[:, b : b + 1],
@@ -308,18 +318,19 @@ def tile_gau_pa_kernel(
             start_rstd(0)
             spread_vectors()
             tile_stats(HALF_TILES)
-            regroup_w(0)
             normalise(0)
             for j in range(HALF_TILES + 1, TOKEN_TILES):
                 tile_stats(j)
             start_rstd(1)
+            regroup_w(0)
             regroup_w(1)
-            quantise_w(0)
+            nc.scalar.activation(out=warm_silu[:], in_=warm[:], func=ACT.Silu)
             group_x(0, 0)
             normalise(1)
             group_x(0, 1)
             quantise_x(0, 0)
             quantise_x(0, 1)
+            quantise_w(0)
             quantise_w(1)
             regroup_w(2)
             prepare_qk()
@@ -346,6 +357,6 @@ def tile_gau_pa_kernel(
             if r + 2 < W_TILES:
                 quantise_w(r + 2)
             project(c, first + 2)
-            project(c, first + 3)
+            project(c, first + 3, pieces=2 if r == ROUNDS - 1 else 1)
             if r % 2 == 0 and r // 2 < HALVES:
                 project_qk(r // 2)

@@ -32,8 +32,7 @@ W_TILES = CHUNKS * PASSES
 ROUNDS = CHUNKS * HALVES
 STAGE_BUFS = 7
 RUN = 4
-SCALAR_COLS = 512
-GPSIMD_COLS = 128
+SCALAR_COLS = 640
 
 B_HIDDEN_AT = 0
 B_QK_AT = 2 * HID
@@ -109,15 +108,10 @@ def tile_gau_pa_kernel(
                 out=grouped[:, 0:SCALAR_COLS, :].rearrange("p (c i) t -> p c t i", i=RUN),
                 in_=raw[:, :, 0:SCALAR_COLS].rearrange("p t (c i) -> p c t i", i=RUN),
             )
-            for lo in range(SCALAR_COLS, CHUNK, GPSIMD_COLS):
-                nc.gpsimd.tensor_scalar(
-                    out=grouped[:, lo : lo + GPSIMD_COLS, :],
-                    in0=raw[:, :, lo : lo + GPSIMD_COLS].rearrange("p t c -> p c t"),
-                    scalar1=1.0,
-                    scalar2=0.0,
-                    op0=ALU.mult,
-                    op1=ALU.add,
-                )
+            nc.vector.tensor_copy(
+                out=grouped[:, SCALAR_COLS:CHUNK, :].rearrange("p (c i) t -> p c t i", i=RUN),
+                in_=raw[:, :, SCALAR_COLS:CHUNK].rearrange("p t (c i) -> p c t i", i=RUN),
+            )
             w_grouped[w] = grouped
 
         def quantise_w(w):

@@ -32,7 +32,8 @@ W_TILES = CHUNKS * PASSES
 ROUNDS = CHUNKS * HALVES
 STAGE_BUFS = 7
 RUN = 4
-SCALAR_COLS = 640
+SCALAR_COLS = 512
+GPSIMD_COLS = 256
 
 B_HIDDEN_AT = 0
 B_QK_AT = 2 * HID
@@ -108,10 +109,15 @@ def tile_gau_pa_kernel(
                 out=grouped[:, 0:SCALAR_COLS, :].rearrange("p (c i) t -> p c t i", i=RUN),
                 in_=raw[:, :, 0:SCALAR_COLS].rearrange("p t (c i) -> p c t i", i=RUN),
             )
-            nc.vector.tensor_copy(
-                out=grouped[:, SCALAR_COLS:CHUNK, :].rearrange("p (c i) t -> p c t i", i=RUN),
-                in_=raw[:, :, SCALAR_COLS:CHUNK].rearrange("p t (c i) -> p c t i", i=RUN),
-            )
+            for lo in range(SCALAR_COLS, CHUNK, GPSIMD_COLS):
+                nc.gpsimd.tensor_scalar(
+                    out=grouped[:, lo : lo + GPSIMD_COLS, :],
+                    in0=raw[:, :, lo : lo + GPSIMD_COLS].rearrange("p t c -> p c t"),
+                    scalar1=1.0,
+                    scalar2=0.0,
+                    op0=ALU.mult,
+                    op1=ALU.add,
+                )
             w_grouped[w] = grouped
 
         def quantise_w(w):
@@ -122,8 +128,10 @@ def tile_gau_pa_kernel(
                 in_=w_grouped[w][:].rearrange("p c t -> p (c t)"),
             )
 
-        def prepare_qk():
+        def group_qk():
             nc.vector.tensor_copy(out=wqk_grouped[:], in_=wqk_raw[:].rearrange("p (g t) n -> p g n t", t=PACK))
+
+        def quantise_qk():
             nc.vector.quantize_mx(
                 out=wqk_codes[:].rearrange("p g n -> p (g n)").bitcast(FP8X4),
                 scales=wqk_scales[:].rearrange("p g n -> p (g n)"),
@@ -248,8 +256,8 @@ def tile_gau_pa_kernel(
             gain_beta = norm_pool.tile([P, 2 * K_BLOCKS], F32)
             nc.scalar.copy(out=gain_beta[:], in_=ln_bank[:, 0 : 2 * K_BLOCKS])
 
-            def spread_vectors():
-                for i in range(VEC_COLS // (2 * BANK)):
+            def spread_vectors(banks):
+                for i in banks:
                     vec_bank = psum.tile([P, 2 * BANK], BF16, tag="bank")
                     for h in range(2):
                         at = (2 * i + h) * BANK
@@ -271,6 +279,8 @@ def tile_gau_pa_kernel(
             def tile_stats(j):
                 for s in range(DIM // BN_WIDTH):
                     nc.vector.bn_stats(out=stats[:, j, s, :], in_=x_sb[:, j, s * BN_WIDTH : (s + 1) * BN_WIDTH])
+
+            def aggregate(j):
                 nc.vector.bn_aggr(out=mean_var[:, j, :], in_=stats[:, j, :, :].rearrange("p s c -> p (s c)"))
 
             def start_rstd(half):
@@ -307,14 +317,23 @@ def tile_gau_pa_kernel(
                         bias=gain_beta[:, K_BLOCKS + b : K_BLOCKS + b + 1],
                     )
 
-            for j in range(HALF_TILES):
+            spread_vectors(range(0, 3))
+            for j in range(0, HALF_TILES, 2):
                 tile_stats(j)
+                tile_stats(j + 1)
+                aggregate(j)
+                aggregate(j + 1)
             start_rstd(0)
-            spread_vectors()
+            spread_vectors(range(3, VEC_COLS // (2 * BANK)))
             tile_stats(HALF_TILES)
             normalise(0)
-            for j in range(HALF_TILES + 1, TOKEN_TILES):
-                tile_stats(j)
+            tile_stats(HALF_TILES + 1)
+            aggregate(HALF_TILES)
+            aggregate(HALF_TILES + 1)
+            tile_stats(HALF_TILES + 2)
+            tile_stats(HALF_TILES + 3)
+            aggregate(HALF_TILES + 2)
+            aggregate(HALF_TILES + 3)
             start_rstd(1)
             regroup_w(0)
             regroup_w(1)
@@ -322,12 +341,13 @@ def tile_gau_pa_kernel(
             group_x(0, 0)
             normalise(1)
             group_x(0, 1)
+            group_qk()
             quantise_x(0, 0)
             quantise_x(0, 1)
             quantise_w(0)
             quantise_w(1)
+            quantise_qk()
             regroup_w(2)
-            prepare_qk()
 
         stage_pool = ctx.enter_context(tc.tile_pool(name="stage", bufs=STAGE_BUFS))
 
@@ -338,9 +358,9 @@ def tile_gau_pa_kernel(
                 regroup_w(r + 3)
             if r % 2 == 1 and r // 2 < HALVES:
                 offset_scale(r // 2)
-            if r == 2 * HALVES - 1:
-                nc.gpsimd.dma_start(out=q_view, in_=q_stage[:])
-                nc.gpsimd.dma_start(out=k_view, in_=k_stage[:])
+            if r == 2 * HALVES:
+                nc.sync.dma_start(out=q_view, in_=q_stage[:])
+                nc.sync.dma_start(out=k_view, in_=k_stage[:])
             project(c, first)
             project(c, first + 1)
             if r == 0:

from contextlib import ExitStack

import concourse.mybir as mybir
from concourse.masks import make_identity

F32 = mybir.dt.float32
BF16 = mybir.dt.bfloat16
U32 = mybir.dt.uint32
U8 = mybir.dt.uint8
I32 = mybir.dt.int32
FP8X4 = mybir.dt.float8_e4m3fn_x4
ALU = mybir.AluOpType
ACT = mybir.ActivationFunctionType

P = 128
PACK = 4
TOKENS = 1024
DIM = 1024
HID = 2048
QK = 128
EPS = 1e-5
PASSES = DIM // (P * PACK)
K_BLOCKS = DIM // P
TOKEN_TILES = TOKENS // P
BANK = 512
HALF_TILES = BANK // P
HALVES = TOKEN_TILES // HALF_TILES
BN_WIDTH = 512
CHUNK = 1024
CHUNKS = 2 * HID // CHUNK
W_TILES = CHUNKS * PASSES
ROUNDS = CHUNKS * HALVES
STAGE_BUFS = 7
RUN = 4
SCALAR_COLS = 512
GPSIMD_COLS = 256

B_HIDDEN_AT = 0
B_QK_AT = 2 * HID
OS_WEIGHT_AT = B_QK_AT + QK
OS_BIAS_AT = OS_WEIGHT_AT + 2 * QK
VEC_COLS = 5 * 1024

FLOPS = 2 * TOKENS * DIM * (2 * HID + QK)


def tile_gau_pa_kernel(
    tc, x, ln_scale, ln_bias, W_hidden, b_hidden, W_qk, b_qk, os_weight, os_bias, out_0, out_1, out_2, out_3
):
    nc = tc.nc
    with ExitStack() as ctx:
        ctx.enter_context(tc.manual_schedule())
        keep = ctx.enter_context(tc.tile_pool(name="keep", bufs=1))
        grouped_pool = ctx.enter_context(tc.tile_pool(name="grouped", bufs=2))
        psum = ctx.enter_context(tc.psum_pool(name="psum", bufs=8))

        x_view = x.flatten_outer_dims().rearrange("(p j) d -> p j d", j=TOKEN_TILES)
        v_view = out_0.flatten_outer_dims().rearrange("(p j) n -> p j n", j=TOKEN_TILES)
        gate_view = out_1.flatten_outer_dims().rearrange("(p j) n -> p j n", j=TOKEN_TILES)
        q_view = out_2.flatten_outer_dims().rearrange("(p j) n -> p j n", j=TOKEN_TILES)
        k_view = out_3.flatten_outer_dims().rearrange("(p j) n -> p j n", j=TOKEN_TILES)
        w_view = W_hidden.rearrange("(g t p) n -> p g t n", g=PASSES, t=PACK)

        vec_all = keep.tile([P, VEC_COLS], BF16)
        xn_t = []
        for half in range(HALVES):
            xn_half = keep.tile([P, K_BLOCKS, BANK], BF16, name="xn_t%d" % half)
            xn_t.append(xn_half)
        x_codes = keep.tile([P, PASSES, TOKENS], U32, align_bytes=64)
        x_scales = keep.tile([P, PASSES, TOKENS], U8, align_bytes=64)
        w_codes = keep.tile([P, PASSES, 2 * HID], U32, align_bytes=64)
        w_scales = keep.tile([P, PASSES, 2 * HID], U8, align_bytes=64)
        wqk_raw = keep.tile([P, PASSES * PACK, QK], BF16)
        wqk_grouped = keep.tile([P, PASSES, QK, PACK], BF16, align_bytes=64)
        wqk_codes = keep.tile([P, PASSES, QK], U32, align_bytes=64)
        wqk_scales = keep.tile([P, PASSES, QK], U8, align_bytes=64)
        qk = keep.tile([P, TOKEN_TILES, QK], F32)
        q_stage = keep.tile([P, TOKEN_TILES, QK], F32)
        k_stage = keep.tile([P, TOKEN_TILES, QK], F32)
        w_raw = {}
        w_grouped = {}
        x_grouped = {}

        def group_x(half, g):
            grouped = grouped_pool.tile([P, BANK, PACK], BF16, name="x_grouped", align_bytes=64)
            nc.vector.tensor_copy(
                out=grouped[:].rearrange("p (c i) t -> p c t i", i=RUN),
                in_=xn_t[half][:, g * PACK : (g + 1) * PACK, :].rearrange("p t (c i) -> p c t i", i=RUN),
            )
            x_grouped[(half, g)] = grouped

        def quantise_x(half, g):
            nc.vector.quantize_mx(
                out=x_codes[:, g, half * BANK : (half + 1) * BANK].bitcast(FP8X4),
                scales=x_scales[:, g, half * BANK : (half + 1) * BANK],
                in_=x_grouped[(half, g)][:].rearrange("p c t -> p (c t)"),
            )

        def load_w(w):
            c, g = w // PASSES, w % PASSES
            raw = keep.tile([P, PACK, CHUNK], BF16, name="raw%d" % w)
            nc.sync.dma_start(out=raw[:], in_=w_view[:, g, :, c * CHUNK : (c + 1) * CHUNK])
            w_raw[w] = raw

        def regroup_w(w):
            raw = w_raw[w]
            grouped = grouped_pool.tile([P, CHUNK, PACK], BF16, name="w_grouped", align_bytes=64)
            nc.scalar.copy(
                out=grouped[:, 0:SCALAR_COLS, :].rearrange("p (c i) t -> p c t i", i=RUN),
                in_=raw[:, :, 0:SCALAR_COLS].rearrange("p t (c i) -> p c t i", i=RUN),
            )
            for lo in range(SCALAR_COLS, CHUNK, GPSIMD_COLS):
                nc.gpsimd.tensor_scalar(
                    out=grouped[:, lo : lo + GPSIMD_COLS, :],
                    in0=raw[:, :, lo : lo + GPSIMD_COLS].rearrange("p t c -> p c t"),
                    scalar1=1.0,
                    scalar2=0.0,
                    op0=ALU.mult,
                    op1=ALU.add,
                )
            w_grouped[w] = grouped

        def quantise_w(w):
            c, g = w // PASSES, w % PASSES
            nc.vector.quantize_mx(
                out=w_codes[:, g, c * CHUNK : (c + 1) * CHUNK].bitcast(FP8X4),
                scales=w_scales[:, g, c * CHUNK : (c + 1) * CHUNK],
                in_=w_grouped[w][:].rearrange("p c t -> p (c t)"),
            )

        def group_qk():
            nc.vector.tensor_copy(out=wqk_grouped[:], in_=wqk_raw[:].rearrange("p (g t) n -> p g n t", t=PACK))

        def quantise_qk():
            nc.vector.quantize_mx(
                out=wqk_codes[:].rearrange("p g n -> p (g n)").bitcast(FP8X4),
                scales=wqk_scales[:].rearrange("p g n -> p (g n)"),
                in_=wqk_grouped[:].rearrange("p g n t -> p (g n t)"),
            )

        def project(c, j, pieces=1):
            banks = []
            for h in range(CHUNK // BANK):
                acc = psum.tile([P, BANK], F32, tag="bank")
                banks.append(acc)
            for g in range(PASSES):
                for h in range(CHUNK // BANK):
                    at = c * CHUNK + h * BANK
                    nc.tensor.matmul_mx(
                        out=banks[h][:],
                        lhsT=x_codes[:, g, j * P : (j + 1) * P].bitcast(FP8X4),
                        lhsT_scale=x_scales[:, g, j * P : (j + 1) * P],
                        rhs=w_codes[:, g, at : at + BANK].bitcast(FP8X4),
                        rhs_scale=w_scales[:, g, at : at + BANK],
                        start=(g == 0),
                        stop=(g == PASSES - 1),
                    )
            stage = stage_pool.tile([P, CHUNK], F32)
            for h in range(CHUNK // BANK):
                at = c * CHUNK + h * BANK
                nc.vector.tensor_tensor(
                    out=stage[:, h * BANK : (h + 1) * BANK],
                    in0=banks[h][:],
                    in1=vec_all[:, B_HIDDEN_AT + at : B_HIDDEN_AT + at + BANK],
                    op=ALU.add,
                )
            dest = v_view if c < CHUNKS // 2 else gate_view
            at = (c % (CHUNKS // 2)) * CHUNK
            width = CHUNK // pieces
            for lo in range(0, CHUNK, width):
                nc.scalar.activation(out=stage[:, lo : lo + width], in_=stage[:, lo : lo + width], func=ACT.Silu)
                nc.sync.dma_start(out=dest[:, j, at + lo : at + lo + width], in_=stage[:, lo : lo + width])

        def along_tiles(at):
            return vec_all[:, at : at + QK].unsqueeze(1).to_broadcast([P, HALF_TILES, QK])

        def project_qk(half):
            these = slice(half * HALF_TILES, (half + 1) * HALF_TILES)
            acc = psum.tile([P, HALF_TILES, QK], F32, tag="bank")
            for i in range(HALF_TILES):
                j = half * HALF_TILES + i
                for g in range(PASSES):
                    nc.tensor.matmul_mx(
                        out=acc[:, i, :],
                        lhsT=x_codes[:, g, j * P : (j + 1) * P].bitcast(FP8X4),
                        lhsT_scale=x_scales[:, g, j * P : (j + 1) * P],
                        rhs=wqk_codes[:, g, :].bitcast(FP8X4),
                        rhs_scale=wqk_scales[:, g, :],
                        start=(g == 0),
                        stop=(g == PASSES - 1),
                    )
            nc.vector.tensor_tensor(out=qk[:, these, :], in0=acc[:], in1=along_tiles(B_QK_AT), op=ALU.add)
            nc.scalar.activation(out=qk[:, these, :], in_=qk[:, these, :], func=ACT.Silu)

        def offset_scale(half):
            these = slice(half * HALF_TILES, (half + 1) * HALF_TILES)
            for a, scaled in enumerate((q_stage, k_stage)):
                nc.gpsimd.tensor_tensor(
                    out=scaled[:, these, :], in0=qk[:, these, :], in1=along_tiles(OS_WEIGHT_AT + a * QK), op=ALU.mult
                )
                nc.gpsimd.tensor_tensor(
                    out=scaled[:, these, :],
                    in0=scaled[:, these, :],
                    in1=along_tiles(OS_BIAS_AT + a * QK),
                    op=ALU.add,
                )

        with tc.tile_pool(name="norm", bufs=1) as norm_pool:
            warm = norm_pool.tile([P, 1], F32)
            nc.vector.memset(warm[:], 1.0)
            warm_sqrt = norm_pool.tile([P, 1], F32)
            nc.scalar.activation(out=warm_sqrt[:], in_=warm[:], func=ACT.Sqrt)
            warm_silu = norm_pool.tile([P, 1], F32)

            ident_bf16 = norm_pool.tile([P, P], BF16)
            make_identity(nc, ident_bf16[:])
            ident_f32 = norm_pool.tile([P, P], F32)
            make_identity(nc, ident_f32[:])
            ln_rows = norm_pool.tile([P, P], BF16)
            nc.vector.memset(ln_rows[:].bitcast(I32), 0)
            vec_rows = norm_pool.tile([P, VEC_COLS], BF16)
            nc.vector.memset(vec_rows[:].bitcast(I32), 0)
            ones = norm_pool.tile([P, P], BF16)
            nc.vector.memset(ones[:], 1.0)

            x_sb = norm_pool.tile([P, TOKEN_TILES, DIM], BF16)

            def load_x(j, tiles):
                nc.sync.dma_start(out=x_sb[:, j : j + tiles, :], in_=x_view[:, j : j + tiles, :])

            load_x(0, 1)
            load_x(1, 1)
            nc.sync.dma_start(out=ln_rows[0:K_BLOCKS, :], in_=ln_scale.rearrange("(b p) -> b p", p=P))
            nc.sync.dma_start(out=ln_rows[K_BLOCKS : 2 * K_BLOCKS, :], in_=ln_bias.rearrange("(b p) -> b p", p=P))
            load_x(2, 2)
            nc.sync.dma_start(out=vec_rows[0:1, B_HIDDEN_AT : B_HIDDEN_AT + 2 * HID], in_=b_hidden.unsqueeze(0))
            nc.sync.dma_start(out=vec_rows[0:1, B_QK_AT : B_QK_AT + QK], in_=b_qk.unsqueeze(0))
            nc.sync.dma_start(
                out=vec_rows[0:1, OS_WEIGHT_AT : OS_WEIGHT_AT + 2 * QK],
                in_=os_weight.rearrange("a n -> (a n)").unsqueeze(0),
            )
            nc.sync.dma_start(
                out=vec_rows[0:1, OS_BIAS_AT : OS_BIAS_AT + 2 * QK],
                in_=os_bias.rearrange("a n -> (a n)").unsqueeze(0),
            )
            load_x(4, 2)
            load_x(6, 2)
            load_w(0)
            load_w(1)
            nc.sync.dma_start(out=wqk_raw[:], in_=W_qk.rearrange("(s p) n -> p s n", p=P))
            for w in range(2, W_TILES):
                load_w(w)

            ln_bank = psum.tile([P, P], BF16, tag="bank")
            nc.tensor.transpose(ln_bank[:], ln_rows[:], ident_bf16[:])
            gain_beta = norm_pool.tile([P, 2 * K_BLOCKS], F32)
            nc.scalar.copy(out=gain_beta[:], in_=ln_bank[:, 0 : 2 * K_BLOCKS])

            def spread_vectors(banks):
                for i in banks:
                    vec_bank = psum.tile([P, 2 * BANK], BF16, tag="bank")
                    for h in range(2):
                        at = (2 * i + h) * BANK
                        nc.tensor.matmul(
                            out=vec_bank[:, h * BANK : (h + 1) * BANK],
                            lhsT=ones[:],
                            rhs=vec_rows[:, at : at + BANK],
                            start=True,
                            stop=True,
                        )
                    nc.scalar.copy(out=vec_all[:, 2 * i * BANK : 2 * (i + 1) * BANK], in_=vec_bank[:])

            stats = norm_pool.tile([P, TOKEN_TILES, DIM // BN_WIDTH, 6], F32)
            mean_var = norm_pool.tile([P, TOKEN_TILES, 2], F32)
            var_eps = norm_pool.tile([P, TOKEN_TILES], F32)
            std = norm_pool.tile([P, TOKEN_TILES], F32)
            rstd = norm_pool.tile([P, TOKEN_TILES], F32)

            def tile_stats(j):
                for s in range(DIM // BN_WIDTH):
                    nc.vector.bn_stats(out=stats[:, j, s, :], in_=x_sb[:, j, s * BN_WIDTH : (s + 1) * BN_WIDTH])

            def aggregate(j):
                nc.vector.bn_aggr(out=mean_var[:, j, :], in_=stats[:, j, :, :].rearrange("p s c -> p (s c)"))

            def start_rstd(half):
                these = slice(half * HALF_TILES, (half + 1) * HALF_TILES)
                nc.vector.tensor_scalar(
                    out=var_eps[:, these], in0=mean_var[:, these, 1], scalar1=EPS, scalar2=None, op0=ALU.add
                )
                nc.scalar.activation(out=std[:, these], in_=var_eps[:, these], func=ACT.Sqrt)

            def normalise(half):
                these = slice(half * HALF_TILES, (half + 1) * HALF_TILES)
                nc.vector.reciprocal(out=rstd[:, these], in_=std[:, these])
                xhat = []
                for j in range(half * HALF_TILES, (half + 1) * HALF_TILES):
                    xh = norm_pool.tile([P, DIM], F32, name="xh", bufs=HALF_TILES)
                    nc.vector.tensor_scalar(
                        out=xh[:],
                        in0=x_sb[:, j, :],
                        scalar1=mean_var[:, j, 0:1],
                        scalar2=rstd[:, j : j + 1],
                        op0=ALU.subtract,
                        op1=ALU.mult,
                    )
                    xhat.append(xh)
                for b in range(K_BLOCKS):
                    t_bank = psum.tile([P, HALF_TILES, P], F32, tag="bank")
                    for i in range(HALF_TILES):
                        nc.tensor.transpose(t_bank[:, i, :], xhat[i][:, b * P : (b + 1) * P], ident_f32[:])
                    nc.scalar.activation(
                        out=xn_t[half][:, b, :],
                        in_=t_bank[:].rearrange("p i r -> p (i r)"),
                        func=ACT.Identity,
                        scale=gain_beta[:, b : b + 1],
                        bias=gain_beta[:, K_BLOCKS + b : K_BLOCKS + b + 1],
                    )

            spread_vectors(range(0, 3))
            for j in range(0, HALF_TILES, 2):
                tile_stats(j)
                tile_stats(j + 1)
                aggregate(j)
                aggregate(j + 1)
            start_rstd(0)
            spread_vectors(range(3, VEC_COLS // (2 * BANK)))
            tile_stats(HALF_TILES)
            normalise(0)
            tile_stats(HALF_TILES + 1)
            aggregate(HALF_TILES)
            aggregate(HALF_TILES + 1)
            tile_stats(HALF_TILES + 2)
            tile_stats(HALF_TILES + 3)
            aggregate(HALF_TILES + 2)
            aggregate(HALF_TILES + 3)
            start_rstd(1)
            regroup_w(0)
            regroup_w(1)
            nc.scalar.activation(out=warm_silu[:], in_=warm[:], func=ACT.Silu)
            group_x(0, 0)
            normalise(1)
            group_x(0, 1)
            group_qk()
            quantise_x(0, 0)
            quantise_x(0, 1)
            quantise_w(0)
            quantise_w(1)
            quantise_qk()
            regroup_w(2)

        stage_pool = ctx.enter_context(tc.tile_pool(name="stage", bufs=STAGE_BUFS))

        for r in range(ROUNDS):
            c, half = r // HALVES, r % HALVES
            first = half * HALF_TILES
            if r + 3 < W_TILES:
                regroup_w(r + 3)
            if r % 2 == 1 and r // 2 < HALVES:
                offset_scale(r // 2)
            if r == 2 * HALVES:
                nc.sync.dma_start(out=q_view, in_=q_stage[:])
                nc.sync.dma_start(out=k_view, in_=k_stage[:])
            project(c, first)
            project(c, first + 1)
            if r == 0:
                for g in range(PASSES):
                    group_x(1, g)
                for g in range(PASSES):
                    quantise_x(1, g)
            if r + 2 < W_TILES:
                quantise_w(r + 2)
            project(c, first + 2)
            project(c, first + 3, pieces=2 if r == ROUNDS - 1 else 1)
            if r % 2 == 0 and r // 2 < HALVES:
                project_qk(r // 2)
